import numpy as np
import ml_dtypes


def mxq(x, axis, fmt="e4m3"):
    dtype, down = {"e4m3": (ml_dtypes.float8_e4m3fn, 7), "e5m2": (ml_dtypes.float8_e5m2, 14)}[fmt]
    v = np.moveaxis(np.asarray(x, np.float32).astype(ml_dtypes.bfloat16).astype(np.float64), axis, -1)
    blocks = v.reshape(v.shape[:-1] + (-1, 32))
    amax = np.abs(blocks).max(-1, keepdims=True)
    byte = np.maximum(np.where(amax > 0, np.frexp(amax)[1] - 1 + 127, 0) - down, 1)
    scale = np.exp2(byte - 127.0)
    codes = (blocks / scale).astype(np.float32).astype(dtype).astype(np.float64)
    return np.moveaxis((codes * scale).reshape(v.shape), -1, axis)


WIDE = False


def mx_kscale(k):
    if not WIDE:
        return np.ones(k)
    levels = np.array([10, -10, 5, -5, 0])
    a = np.random.permutation(np.resize(levels, k // 512 * 4)).reshape(k // 512, 4)
    idx = np.arange(k)
    return np.exp2(a[idx // 512, idx % 128 // 32])


BF16 = ml_dtypes.bfloat16


def bf(x):
    return np.asarray(x, np.float32).astype(BF16)


def f64(x):
    return np.asarray(x).astype(np.float64)


B, S, DIM, H, DH, DV, R = 2, 2048, 512, 4, 128, 128, 512
EPS = 1e-6
N = H * (DH + DV)


def rmsnorm(c, w):
    norm = np.mean(c * c, axis=-1, keepdims=True)
    return w * (c * (1.0 / np.sqrt(norm + EPS)))


def setup_inputs():
    s, t = mx_kscale(DIM), mx_kscale(R)
    return {"x": bf(np.random.standard_normal((B, S, DIM)) * s),
            "wkv_a_w": bf(np.random.standard_normal((R, DIM)) / np.sqrt(DIM) / s[None, :]),
            "wkv_a_b": bf(np.random.standard_normal(R) * 0.3),
            "kv_norm_w": bf((1.0 + 0.1 * np.random.standard_normal(R)) * t),
            "wkv_b_w": bf(np.random.standard_normal((N, R)) / np.sqrt(R) / t[None, :]),
            "wkv_b_b": bf(np.random.standard_normal(N) * 0.3)}


def reference(x, wkv_a_w, wkv_a_b, kv_norm_w, wkv_b_w, wkv_b_b):
    c = (mxq(f64(x), 2, "e4m3") @ mxq(f64(wkv_a_w), 1, "e4m3").T) + f64(wkv_a_b)
    kv_c = rmsnorm(c, f64(kv_norm_w))
    kv = (mxq(kv_c, 2, "e4m3") @ mxq(f64(wkv_b_w), 1, "e4m3").T) + f64(wkv_b_b)
    kv = kv.reshape(B, S, H, DH + DV)
    return kv[..., :DH], kv[..., DH:]

@@ -1,0 +1,297 @@
+from contextlib import ExitStack
+
+import concourse.mybir as mybir
+from concourse.masks import make_identity
+
+F32 = mybir.dt.float32
+BF16 = mybir.dt.bfloat16
+U32 = mybir.dt.uint32
+U8 = mybir.dt.uint8
+FP8X4 = mybir.dt.float8_e4m3fn_x4
+ADD = mybir.AluOpType.add
+MULT = mybir.AluOpType.mult
+ACT = mybir.ActivationFunctionType
+
+P = 128
+PACK = 4
+HALVES = 2
+TOKENS = 4096
+K = 512
+HEADS = 4
+HEAD = 128
+KV = 2
+EPS = 1e-6
+
+GROUP_TILES = 4
+GROUPS = TOKENS // (P * GROUP_TILES)
+ROUND_TILES = 2
+ROUNDS = TOKENS // (P * ROUND_TILES)
+ROUND_COLS = ROUND_TILES * P
+
+FLOPS = 2 * TOKENS * K * K + 2 * TOKENS * K * (HEADS * KV * HEAD)
+
+
+def block(i, width):
+    return slice(i * width, (i + 1) * width)
+
+
+def live(r):
+    return 0 <= r < ROUNDS
+
+
+def tile_mla_pa_t_kernel(
+    tc, x, wkv_a_w, wkv_a_b, kv_norm_w, wkv_b_w, wkv_b_b, out_0, out_1
+):
+    nc = tc.nc
+    x_groups = x.flatten_outer_dims().rearrange("(g p i) d -> g p (i d)", p=P, i=GROUP_TILES)
+    out_groups = [
+        o.rearrange("b s h c -> (b s) (h c)").rearrange("(g p i) n -> g p i n", p=P, i=GROUP_TILES)
+        for o in (out_0, out_1)
+    ]
+
+    with ExitStack() as stack:
+        keep = stack.enter_context(tc.tile_pool(name="keep", bufs=1))
+        work = stack.enter_context(tc.tile_pool(name="work", bufs=2))
+        scrap = stack.enter_context(tc.tile_pool(name="scrap", bufs=4))
+        stage = stack.enter_context(tc.tile_pool(name="stage", bufs=4))
+        psum_t = stack.enter_context(tc.psum_pool(name="psum_t", bufs=1))
+        psum_c = stack.enter_context(tc.psum_pool(name="psum_c", bufs=ROUND_TILES))
+        psum_o = stack.enter_context(tc.psum_pool(name="psum_o", bufs=ROUND_TILES * KV))
+        stack.enter_context(tc.manual_schedule())
+
+        wa_sb = keep.tile([P, K // P, K], BF16)
+        wb_sb = keep.tile([P, HEADS, KV, K], BF16)
+        x_sb = keep.tile([P, GROUPS, GROUP_TILES * K], BF16)
+        nc.sync.dma_start(out=wa_sb[:], in_=wkv_a_w.rearrange("(m p) d -> p m d", p=P))
+        nc.sync.dma_start(out=x_sb[:, 0, :], in_=x_groups[0])
+        wb_heads = wkv_b_w.rearrange("(h s p) r -> h p s r", s=KV, p=P)
+        for h in range(HEADS):
+            nc.sync.dma_start(out=wb_sb[:, h], in_=wb_heads[h])
+        for g in range(1, GROUPS):
+            nc.sync.dma_start(out=x_sb[:, g, :], in_=x_groups[g])
+        bias_a = keep.tile([P, K], BF16)
+        gain = keep.tile([P, K], BF16)
+        bias_b = keep.tile([P, HEADS, KV, HEAD], BF16)
+        nc.scalar.dma_start(out=bias_a[:], in_=wkv_a_b.partition_broadcast(P))
+        nc.scalar.dma_start(out=gain[:], in_=kv_norm_w.partition_broadcast(P))
+        nc.scalar.dma_start(
+            out=bias_b[:].rearrange("p h s c -> p (h s c)"), in_=wkv_b_b.partition_broadcast(P)
+        )
+
+        ident = keep.tile([P, P], F32)
+        make_identity(nc, ident[:])
+        one = keep.tile([P, 1], F32)
+        nc.vector.memset(one[:], 1.0)
+        nc.scalar.activation(out=one[:], in_=one[:], func=ACT.Sqrt)
+        eps = keep.tile([P, 1], F32)
+        nc.vector.memset(eps[:], EPS)
+
+        def transpose_words(bank, rows):
+            for s in range(len(rows)):
+                words = rows[s].bitcast(F32)
+                for u in range(HALVES):
+                    nc.tensor.transpose(bank[:, s, u, :], words[:, block(u, P)], ident[:])
+
+        def pair_halves(bank):
+            return bank[:].rearrange("p s u r -> p s r u")
+
+        wa_grouped = keep.tile([P, K, PACK], BF16, align_bytes=64)
+        wa_codes = keep.tile([P, K], U32, align_bytes=64)
+        wa_scales = keep.tile([P, K], U8, align_bytes=64)
+        for b in range(2):
+            wa_bank = psum_o.tile([P, 2, HALVES, P], F32, tag="o")
+            transpose_words(wa_bank, [wa_sb[:, 2 * b + s, :] for s in range(2)])
+            nc.vector.tensor_copy(
+                out=wa_grouped[:, block(b, 2 * P), :]
+                .bitcast(F32)
+                .rearrange("p (s r) u -> p s r u", s=2),
+                in_=pair_halves(wa_bank),
+            )
+        nc.vector.quantize_mx(
+            out=wa_codes[:].bitcast(FP8X4),
+            scales=wa_scales[:],
+            in_=wa_grouped[:].rearrange("p r j -> p (r j)"),
+        )
+
+        wb_codes = keep.tile([P, KV, HEADS, HEAD], U32, align_bytes=64)
+        wb_scales = keep.tile([P, KV, HEADS, HEAD], U8, align_bytes=64)
+        wb_banks = {}
+
+        def transpose_wb(h):
+            wb_banks[h] = psum_o.tile([P, KV, HALVES, P], F32, tag="o", name="wb_bank")
+            transpose_words(wb_banks[h], [wb_sb[:, h, s, :] for s in range(KV)])
+
+        def quantise_wb(h):
+            wb_grouped = work.tile([P, KV, HEAD, PACK], BF16, align_bytes=64)
+            nc.vector.tensor_copy(out=wb_grouped[:].bitcast(F32), in_=pair_halves(wb_banks[h]))
+            for s in range(KV):
+                nc.vector.quantize_mx(
+                    out=wb_codes[:, s, h, :].bitcast(FP8X4),
+                    scales=wb_scales[:, s, h, :],
+                    in_=wb_grouped[:, s].rearrange("p r j -> p (r j)"),
+                )
+
+        x_bank, x_grouped, x_codes, x_scales = {}, {}, {}, {}
+        c_bank, c_biased, c_gained, rstd = {}, {}, {}, {}
+        l_rows, l_bank, l_grouped, l_codes, l_scales = {}, {}, {}, {}, {}
+        o_bank = {}
+
+        def transpose_x(r):
+            g, first = divmod(r * ROUND_TILES, GROUP_TILES)
+            x_bank[r] = psum_t.tile([P, ROUND_TILES, HALVES, P], F32, name="x_bank")
+            transpose_words(
+                x_bank[r], [x_sb[:, g, block(first + s, K)] for s in range(ROUND_TILES)]
+            )
+
+        def regroup_x(r):
+            x_grouped[r] = work.tile(
+                [P, ROUND_TILES, P, PACK], BF16, align_bytes=64, name="x_grouped"
+            )
+            nc.scalar.copy(out=x_grouped[r][:].bitcast(F32), in_=pair_halves(x_bank[r]))
+
+        def quantise(grouped, codes, scales):
+            nc.vector.quantize_mx(
+                out=codes[:].bitcast(FP8X4),
+                scales=scales[:],
+                in_=grouped[:].rearrange("p s t j -> p (s t j)"),
+            )
+
+        def quantise_x(r):
+            x_codes[r] = work.tile([P, ROUND_COLS], U32, align_bytes=64, name="x_codes")
+            x_scales[r] = work.tile([P, ROUND_COLS], U8, align_bytes=64, name="x_scales")
+            quantise(x_grouped[r], x_codes[r], x_scales[r])
+
+        def first_matmul(r):
+            for s in range(ROUND_TILES):
+                c_bank[r, s] = psum_c.tile([P, K], F32, name="c_bank")
+                nc.tensor.matmul_mx(
+                    out=c_bank[r, s][:],
+                    lhsT=x_codes[r][:, block(s, P)].bitcast(FP8X4),
+                    lhsT_scale=x_scales[r][:, block(s, P)],
+                    rhs=wa_codes[:].bitcast(FP8X4),
+                    rhs_scale=wa_scales[:],
+                    start=True,
+                    stop=True,
+                )
+
+        def add_first_bias(r):
+            c_biased[r] = work.tile([P, ROUND_TILES, K], F32, name="c_biased")
+            for s in range(ROUND_TILES):
+                nc.vector.tensor_tensor(
+                    out=c_biased[r][:, s, :], in0=c_bank[r, s][:], in1=bias_a[:], op=ADD
+                )
+
+        def apply_gain(r):
+            c_gained[r] = work.tile([P, ROUND_TILES, K], F32, name="c_gained")
+            for s in range(ROUND_TILES):
+                nc.gpsimd.tensor_tensor(
+                    out=c_gained[r][:, s, :], in0=c_biased[r][:, s, :], in1=gain[:], op=MULT
+                )
+
+        def root_mean_square(r):
+            sum_sq = work.tile([P, ROUND_TILES], F32, name="sum_sq")
+            for s in range(ROUND_TILES):
+                squares = scrap.tile([P, K], BF16, name="squares")
+                nc.scalar.activation(
+                    out=squares[:],
+                    in_=c_biased[r][:, s, :],
+                    func=ACT.Square,
+                    accum_out=sum_sq[:, s : s + 1],
+                )
+            rms = work.tile([P, ROUND_TILES], F32, name="rms")
+            nc.scalar.activation(
+                out=rms[:], in_=sum_sq[:], func=ACT.Sqrt, scale=1.0 / K, bias=eps[:]
+            )
+            return rms
+
+        def invert(r, rms):
+            rstd[r] = work.tile([P, ROUND_TILES], F32, name="rstd")
+            nc.vector.reciprocal(out=rstd[r][:], in_=rms[:])
+
+        def normalise(r):
+            l_rows[r] = work.tile([P, ROUND_TILES, K], BF16, name="l_rows")
+            for s in range(ROUND_TILES):
+                nc.scalar.activation(
+                    out=l_rows[r][:, s, :],
+                    in_=c_gained[r][:, s, :],
+                    func=ACT.Copy,
+                    scale=rstd[r][:, s : s + 1],
+                )
+
+        def transpose_latent(r):
+            l_bank[r] = psum_t.tile([P, ROUND_TILES, HALVES, P], F32, name="l_bank")
+            transpose_words(l_bank[r], [l_rows[r][:, s, :] for s in range(ROUND_TILES)])
+
+        def regroup_latent(r):
+            l_grouped[r] = work.tile(
+                [P, ROUND_TILES, P, PACK], BF16, align_bytes=64, name="l_grouped"
+            )
+            nc.scalar.copy(out=l_grouped[r][:].bitcast(F32), in_=pair_halves(l_bank[r]))
+
+        def quantise_latent(r):
+            l_codes[r] = work.tile([P, ROUND_COLS], U32, align_bytes=64, name="l_codes")
+            l_scales[r] = work.tile([P, ROUND_COLS], U8, align_bytes=64, name="l_scales")
+            quantise(l_grouped[r], l_codes[r], l_scales[r])
+
+        def second_matmul(r):
+            for s in range(ROUND_TILES):
+                for kv in range(KV):
+                    o_bank[r, s, kv] = psum_o.tile([P, HEADS, HEAD], F32, tag="o", name="o_bank")
+                    nc.tensor.matmul_mx(
+                        out=o_bank[r, s, kv][:].rearrange("p h c -> p (h c)"),
+                        lhsT=l_codes[r][:, block(s, P)].bitcast(FP8X4),
+                        lhsT_scale=l_scales[r][:, block(s, P)],
+                        rhs=wb_codes[:, kv].rearrange("p h c -> p (h c)").bitcast(FP8X4),
+                        rhs_scale=wb_scales[:, kv].rearrange("p h c -> p (h c)"),
+                        start=True,
+                        stop=True,
+                    )
+
+        def add_second_bias_and_store(r):
+            g, first = divmod(r * ROUND_TILES, GROUP_TILES)
+            result = stage.tile([P, KV, ROUND_TILES, HEADS, HEAD], F32, name="result")
+            for s in range(ROUND_TILES):
+                for kv in range(KV):
+                    nc.vector.tensor_tensor(
+                        out=result[:, kv, s], in0=o_bank[r, s, kv][:], in1=bias_b[:, :, kv, :], op=ADD
+                    )
+            for kv in range(KV):
+                nc.sync.dma_start(
+                    out=out_groups[kv][g][:, first : first + ROUND_TILES, :],
+                    in_=result[:, kv].rearrange("p s h c -> p s (h c)"),
+                )
+
+        X_AHEAD = 3
+        WB_FIRST = -2
+        for n in range(-X_AHEAD, ROUNDS + 2):
+            h = n - WB_FIRST
+            if live(n):
+                add_first_bias(n)
+            if live(n - 1):
+                normalise(n - 1)
+            if live(n - 2):
+                second_matmul(n - 2)
+            if live(n + 1):
+                first_matmul(n + 1)
+            if live(n - 1):
+                transpose_latent(n - 1)
+            if live(n + X_AHEAD):
+                transpose_x(n + X_AHEAD)
+            if 0 <= h < HEADS:
+                transpose_wb(h)
+            if live(n):
+                apply_gain(n)
+            if live(n - 2):
+                add_second_bias_and_store(n - 2)
+            if live(n):
+                invert(n, root_mean_square(n))
+            if live(n - 1):
+                regroup_latent(n - 1)
+            if live(n + X_AHEAD):
+                regroup_x(n + X_AHEAD)
+            if live(n + 2):
+                quantise_x(n + 2)
+            if live(n - 1):
+                quantise_latent(n - 1)
+            if 0 <= h < HEADS:
+                quantise_wb(h)

@@ -28,6 +28,11 @@ ROUND_TILES = 2
 ROUNDS = TOKENS // (P * ROUND_TILES)
 ROUND_COLS = ROUND_TILES * P
 
+BIAS_A = 0
+GAIN = K
+BIAS_B = 2 * K
+VECTOR_COLS = 2 * K + HEADS * KV * HEAD
+
 FLOPS = 2 * TOKENS * K * K + 2 * TOKENS * K * (HEADS * KV * HEAD)
 
 
@@ -59,6 +64,13 @@ def tile_mla_pa_t_kernel(
         psum_o = stack.enter_context(tc.psum_pool(name="psum_o", bufs=ROUND_TILES * KV))
         stack.enter_context(tc.manual_schedule())
 
+        vectors = keep.tile([P, VECTOR_COLS], BF16)
+        nc.vector.memset(vectors[:], 0.0)
+        for first, vector in ((BIAS_A, wkv_a_b), (GAIN, kv_norm_w), (BIAS_B, wkv_b_b)):
+            nc.sync.dma_start(
+                out=vectors[0:1, first : first + vector.shape[0]],
+                in_=vector.rearrange("(o n) -> o n", o=1),
+            )
         wa_sb = keep.tile([P, K // P, K], BF16)
         wb_sb = keep.tile([P, HEADS, KV, K], BF16)
         x_sb = keep.tile([P, GROUPS, GROUP_TILES * K], BF16)
@@ -69,14 +81,6 @@ def tile_mla_pa_t_kernel(
             nc.sync.dma_start(out=wb_sb[:, h], in_=wb_heads[h])
         for g in range(1, GROUPS):
             nc.sync.dma_start(out=x_sb[:, g, :], in_=x_groups[g])
-        bias_a = keep.tile([P, K], BF16)
-        gain = keep.tile([P, K], BF16)
-        bias_b = keep.tile([P, HEADS, KV, HEAD], BF16)
-        nc.scalar.dma_start(out=bias_a[:], in_=wkv_a_b.partition_broadcast(P))
-        nc.scalar.dma_start(out=gain[:], in_=kv_norm_w.partition_broadcast(P))
-        nc.scalar.dma_start(
-            out=bias_b[:].rearrange("p h s c -> p (h s c)"), in_=wkv_b_b.partition_broadcast(P)
-        )
 
         ident = keep.tile([P, P], F32)
         make_identity(nc, ident[:])
@@ -85,6 +89,19 @@ def tile_mla_pa_t_kernel(
         nc.scalar.activation(out=one[:], in_=one[:], func=ACT.Sqrt)
         eps = keep.tile([P, 1], F32)
         nc.vector.memset(eps[:], EPS)
+
+        ones = keep.tile([P, P], BF16)
+        nc.vector.memset(ones[:], 1.0)
+        spread = keep.tile([P, VECTOR_COLS], BF16)
+        for b in range(VECTOR_COLS // K):
+            spread_bank = psum_o.tile([P, K], F32, tag="o")
+            nc.tensor.matmul(
+                out=spread_bank[:], lhsT=ones[:], rhs=vectors[:, block(b, K)], start=True, stop=True
+            )
+            nc.vector.tensor_copy(out=spread[:, block(b, K)], in_=spread_bank[:])
+        bias_a = spread[:, BIAS_A : BIAS_A + K]
+        gain = spread[:, GAIN : GAIN + K]
+        bias_b = spread[:, BIAS_B:VECTOR_COLS].rearrange("p (h s c) -> p h s c", h=HEADS, s=KV)
 
         def transpose_words(bank, rows):
             for s in range(len(rows)):
@@ -101,7 +118,7 @@ def tile_mla_pa_t_kernel(
         for b in range(2):
             wa_bank = psum_o.tile([P, 2, HALVES, P], F32, tag="o")
             transpose_words(wa_bank, [wa_sb[:, 2 * b + s, :] for s in range(2)])
-            nc.vector.tensor_copy(
+            nc.scalar.copy(
                 out=wa_grouped[:, block(b, 2 * P), :]
                 .bitcast(F32)
                 .rearrange("p (s r) u -> p s r u", s=2),
@@ -178,14 +195,14 @@ def tile_mla_pa_t_kernel(
             c_biased[r] = work.tile([P, ROUND_TILES, K], F32, name="c_biased")
             for s in range(ROUND_TILES):
                 nc.vector.tensor_tensor(
-                    out=c_biased[r][:, s, :], in0=c_bank[r, s][:], in1=bias_a[:], op=ADD
+                    out=c_biased[r][:, s, :], in0=c_bank[r, s][:], in1=bias_a, op=ADD
                 )
 
         def apply_gain(r):
             c_gained[r] = work.tile([P, ROUND_TILES, K], F32, name="c_gained")
             for s in range(ROUND_TILES):
                 nc.gpsimd.tensor_tensor(
-                    out=c_gained[r][:, s, :], in0=c_biased[r][:, s, :], in1=gain[:], op=MULT
+                    out=c_gained[r][:, s, :], in0=c_biased[r][:, s, :], in1=gain, op=MULT
                 )
 
         def root_mean_square(r):
@@ -234,8 +251,8 @@ def tile_mla_pa_t_kernel(
             quantise(l_grouped[r], l_codes[r], l_scales[r])
 
         def second_matmul(r):
-            for s in range(ROUND_TILES):
-                for kv in range(KV):
+            for kv in range(KV):
+                for s in range(ROUND_TILES):
                     o_bank[r, s, kv] = psum_o.tile([P, HEADS, HEAD], F32, tag="o", name="o_bank")
                     nc.tensor.matmul_mx(
                         out=o_bank[r, s, kv][:].rearrange("p h c -> p (h c)"),
@@ -250,21 +267,18 @@ def tile_mla_pa_t_kernel(
         def add_second_bias_and_store(r):
             g, first = divmod(r * ROUND_TILES, GROUP_TILES)
             result = stage.tile([P, KV, ROUND_TILES, HEADS, HEAD], F32, name="result")
-            for s in range(ROUND_TILES):
-                for kv in range(KV):
+            for kv in range(KV):
+                for s in range(ROUND_TILES):
                     nc.vector.tensor_tensor(
                         out=result[:, kv, s], in0=o_bank[r, s, kv][:], in1=bias_b[:, :, kv, :], op=ADD
                     )
-            for kv in range(KV):
                 nc.sync.dma_start(
                     out=out_groups[kv][g][:, first : first + ROUND_TILES, :],
                     in_=result[:, kv].rearrange("p s h c -> p s (h c)"),
                 )
 
         X_AHEAD = 3
-        WB_FIRST = -2
         for n in range(-X_AHEAD, ROUNDS + 2):
-            h = n - WB_FIRST
             if live(n):
                 add_first_bias(n)
             if live(n - 1):
@@ -277,12 +291,14 @@ def tile_mla_pa_t_kernel(
                 transpose_latent(n - 1)
             if live(n + X_AHEAD):
                 transpose_x(n + X_AHEAD)
-            if 0 <= h < HEADS:
-                transpose_wb(h)
+            if n + X_AHEAD < HEADS:
+                transpose_wb(n + X_AHEAD)
             if live(n):
                 apply_gain(n)
             if live(n - 2):
                 add_second_bias_and_store(n - 2)
+            if 0 <= n + 2 < HEADS:
+                quantise_wb(n + 2)
             if live(n):
                 invert(n, root_mean_square(n))
             if live(n - 1):
@@ -293,5 +309,3 @@ def tile_mla_pa_t_kernel(
                 quantise_x(n + 2)
             if live(n - 1):
                 quantise_latent(n - 1)
-            if 0 <= h < HEADS:
-                quantise_wb(h)

@@ -7,6 +7,7 @@ F32 = mybir.dt.float32
 BF16 = mybir.dt.bfloat16
 U32 = mybir.dt.uint32
 U8 = mybir.dt.uint8
+I32 = mybir.dt.int32
 FP8X4 = mybir.dt.float8_e4m3fn_x4
 ADD = mybir.AluOpType.add
 MULT = mybir.AluOpType.mult
@@ -58,19 +59,11 @@ def tile_mla_pa_t_kernel(
         keep = stack.enter_context(tc.tile_pool(name="keep", bufs=1))
         work = stack.enter_context(tc.tile_pool(name="work", bufs=2))
         scrap = stack.enter_context(tc.tile_pool(name="scrap", bufs=4))
-        stage = stack.enter_context(tc.tile_pool(name="stage", bufs=4))
+        stage = stack.enter_context(tc.tile_pool(name="stage", bufs=8))
         psum_t = stack.enter_context(tc.psum_pool(name="psum_t", bufs=1))
         psum_c = stack.enter_context(tc.psum_pool(name="psum_c", bufs=ROUND_TILES))
         psum_o = stack.enter_context(tc.psum_pool(name="psum_o", bufs=ROUND_TILES * KV))
-        stack.enter_context(tc.manual_schedule())
 
-        vectors = keep.tile([P, VECTOR_COLS], BF16)
-        nc.vector.memset(vectors[:], 0.0)
-        for first, vector in ((BIAS_A, wkv_a_b), (GAIN, kv_norm_w), (BIAS_B, wkv_b_b)):
-            nc.sync.dma_start(
-                out=vectors[0:1, first : first + vector.shape[0]],
-                in_=vector.rearrange("(o n) -> o n", o=1),
-            )
         wa_sb = keep.tile([P, K // P, K], BF16)
         wb_sb = keep.tile([P, HEADS, KV, K], BF16)
         x_sb = keep.tile([P, GROUPS, GROUP_TILES * K], BF16)
@@ -82,26 +75,37 @@ def tile_mla_pa_t_kernel(
         for g in range(1, GROUPS):
             nc.sync.dma_start(out=x_sb[:, g, :], in_=x_groups[g])
 
-        ident = keep.tile([P, P], F32)
-        make_identity(nc, ident[:])
         one = keep.tile([P, 1], F32)
         nc.vector.memset(one[:], 1.0)
         nc.scalar.activation(out=one[:], in_=one[:], func=ACT.Sqrt)
         eps = keep.tile([P, 1], F32)
         nc.vector.memset(eps[:], EPS)
+        ident = keep.tile([P, P], F32)
+        make_identity(nc, ident[:])
 
+        vectors = keep.tile([P, VECTOR_COLS], BF16)
+        nc.vector.memset(vectors[:].bitcast(I32), 0)
+        for first, vector in ((BIAS_A, wkv_a_b), (GAIN, kv_norm_w), (BIAS_B, wkv_b_b)):
+            nc.scalar.dma_start(
+                out=vectors[0:1, first : first + vector.shape[0]],
+                in_=vector.rearrange("(o n) -> o n", o=1),
+            )
         ones = keep.tile([P, P], BF16)
         nc.vector.memset(ones[:], 1.0)
         spread = keep.tile([P, VECTOR_COLS], BF16)
-        for b in range(VECTOR_COLS // K):
-            spread_bank = psum_o.tile([P, K], F32, tag="o")
-            nc.tensor.matmul(
-                out=spread_bank[:], lhsT=ones[:], rhs=vectors[:, block(b, K)], start=True, stop=True
-            )
-            nc.vector.tensor_copy(out=spread[:, block(b, K)], in_=spread_bank[:])
         bias_a = spread[:, BIAS_A : BIAS_A + K]
         gain = spread[:, GAIN : GAIN + K]
         bias_b = spread[:, BIAS_B:VECTOR_COLS].rearrange("p (h s c) -> p h s c", h=HEADS, s=KV)
+        spread_banks = {}
+
+        def spread_on_tensor(b):
+            spread_banks[b] = psum_o.tile([P, K], F32, tag="o", name="spread_bank")
+            nc.tensor.matmul(
+                out=spread_banks[b][:], lhsT=ones[:], rhs=vectors[:, block(b, K)], start=True, stop=True
+            )
+
+        def spread_on_vector(b):
+            nc.vector.tensor_copy(out=spread[:, block(b, K)], in_=spread_banks[b][:])
 
         def transpose_words(bank, rows):
             for s in range(len(rows)):
@@ -149,7 +153,7 @@ def tile_mla_pa_t_kernel(
                 )
 
         x_bank, x_grouped, x_codes, x_scales = {}, {}, {}, {}
-        c_bank, c_biased, c_gained, rstd = {}, {}, {}, {}
+        c_bank, c_biased, c_gained, rms, rstd = {}, {}, {}, {}, {}
         l_rows, l_bank, l_grouped, l_codes, l_scales = {}, {}, {}, {}, {}
         o_bank = {}
 
@@ -215,15 +219,14 @@ def tile_mla_pa_t_kernel(
                     func=ACT.Square,
                     accum_out=sum_sq[:, s : s + 1],
                 )
-            rms = work.tile([P, ROUND_TILES], F32, name="rms")
+            rms[r] = work.tile([P, ROUND_TILES], F32, name="rms")
             nc.scalar.activation(
-                out=rms[:], in_=sum_sq[:], func=ACT.Sqrt, scale=1.0 / K, bias=eps[:]
+                out=rms[r][:], in_=sum_sq[:], func=ACT.Sqrt, scale=1.0 / K, bias=eps[:]
             )
-            return rms
 
-        def invert(r, rms):
+        def invert(r):
             rstd[r] = work.tile([P, ROUND_TILES], F32, name="rstd")
-            nc.vector.reciprocal(out=rstd[r][:], in_=rms[:])
+            nc.vector.reciprocal(out=rstd[r][:], in_=rms[r][:])
 
         def normalise(r):
             l_rows[r] = work.tile([P, ROUND_TILES, K], BF16, name="l_rows")
@@ -264,48 +267,59 @@ def tile_mla_pa_t_kernel(
                         stop=True,
                     )
 
-        def add_second_bias_and_store(r):
+        def add_second_bias_and_store(r, kv):
             g, first = divmod(r * ROUND_TILES, GROUP_TILES)
-            result = stage.tile([P, KV, ROUND_TILES, HEADS, HEAD], F32, name="result")
-            for kv in range(KV):
-                for s in range(ROUND_TILES):
-                    nc.vector.tensor_tensor(
-                        out=result[:, kv, s], in0=o_bank[r, s, kv][:], in1=bias_b[:, :, kv, :], op=ADD
-                    )
-                nc.sync.dma_start(
-                    out=out_groups[kv][g][:, first : first + ROUND_TILES, :],
-                    in_=result[:, kv].rearrange("p s h c -> p s (h c)"),
+            result = stage.tile([P, ROUND_TILES, HEADS, HEAD], F32, name="result")
+            for s in range(ROUND_TILES):
+                nc.vector.tensor_tensor(
+                    out=result[:, s], in0=o_bank[r, s, kv][:], in1=bias_b[:, :, kv, :], op=ADD
                 )
+            nc.sync.dma_start(
+                out=out_groups[kv][g][:, first : first + ROUND_TILES, :],
+                in_=result[:].rearrange("p s h c -> p s (h c)"),
+            )
 
-        X_AHEAD = 3
-        for n in range(-X_AHEAD, ROUNDS + 2):
-            if live(n):
-                add_first_bias(n)
-            if live(n - 1):
-                normalise(n - 1)
-            if live(n - 2):
-                second_matmul(n - 2)
-            if live(n + 1):
-                first_matmul(n + 1)
+        for n in range(-3, ROUNDS + 2):
             if live(n - 1):
                 transpose_latent(n - 1)
-            if live(n + X_AHEAD):
-                transpose_x(n + X_AHEAD)
-            if n + X_AHEAD < HEADS:
-                transpose_wb(n + X_AHEAD)
-            if live(n):
-                apply_gain(n)
             if live(n - 2):
-                add_second_bias_and_store(n - 2)
-            if 0 <= n + 2 < HEADS:
-                quantise_wb(n + 2)
+                second_matmul(n - 2)
+            elif n == -2:
+                spread_on_tensor(0)
+                spread_on_tensor(1)
+            elif n >= 0:
+                transpose_wb(2 * n)
+                transpose_wb(2 * n + 1)
+                spread_on_tensor(2 + n)
+            if live(n + 2):
+                regroup_x(n + 2)
             if live(n):
-                invert(n, root_mean_square(n))
-            if live(n - 1):
-                regroup_latent(n - 1)
-            if live(n + X_AHEAD):
-                regroup_x(n + X_AHEAD)
+                add_first_bias(n)
+            if live(n + 1):
+                first_matmul(n + 1)
+            if live(n + 3):
+                transpose_x(n + 3)
             if live(n + 2):
                 quantise_x(n + 2)
+            if live(n):
+                apply_gain(n)
+                root_mean_square(n)
+            if live(n - 2):
+                add_second_bias_and_store(n - 2, 0)
+            elif n == -2:
+                spread_on_vector(0)
+                spread_on_vector(1)
+            elif n >= 0:
+                quantise_wb(2 * n)
+                quantise_wb(2 * n + 1)
+                spread_on_vector(2 + n)
+            if live(n):
+                invert(n)
+            if live(n - 2):
+                add_second_bias_and_store(n - 2, 1)
+            if live(n - 1):
+                regroup_latent(n - 1)
+            if live(n):
+                normalise(n)
             if live(n - 1):
                 quantise_latent(n - 1)

@@ -63,6 +63,7 @@ def tile_mla_pa_t_kernel(
         psum_t = stack.enter_context(tc.psum_pool(name="psum_t", bufs=1))
         psum_c = stack.enter_context(tc.psum_pool(name="psum_c", bufs=ROUND_TILES))
         psum_o = stack.enter_context(tc.psum_pool(name="psum_o", bufs=ROUND_TILES * KV))
+        stack.enter_context(tc.manual_schedule())
 
         wa_sb = keep.tile([P, K // P, K], BF16)
         wb_sb = keep.tile([P, HEADS, KV, K], BF16)
@@ -280,8 +281,10 @@ def tile_mla_pa_t_kernel(
             )
 
         for n in range(-3, ROUNDS + 2):
+            if live(n):
+                add_first_bias(n)
             if live(n - 1):
-                transpose_latent(n - 1)
+                normalise(n - 1)
             if live(n - 2):
                 second_matmul(n - 2)
             elif n == -2:
@@ -291,21 +294,17 @@ def tile_mla_pa_t_kernel(
                 transpose_wb(2 * n)
                 transpose_wb(2 * n + 1)
                 spread_on_tensor(2 + n)
-            if live(n + 2):
-                regroup_x(n + 2)
-            if live(n):
-                add_first_bias(n)
             if live(n + 1):
                 first_matmul(n + 1)
+            if live(n - 1):
+                transpose_latent(n - 1)
             if live(n + 3):
                 transpose_x(n + 3)
-            if live(n + 2):
-                quantise_x(n + 2)
             if live(n):
                 apply_gain(n)
-                root_mean_square(n)
             if live(n - 2):
                 add_second_bias_and_store(n - 2, 0)
+                add_second_bias_and_store(n - 2, 1)
             elif n == -2:
                 spread_on_vector(0)
                 spread_on_vector(1)
@@ -314,12 +313,13 @@ def tile_mla_pa_t_kernel(
                 quantise_wb(2 * n + 1)
                 spread_on_vector(2 + n)
             if live(n):
+                root_mean_square(n)
                 invert(n)
-            if live(n - 2):
-                add_second_bias_and_store(n - 2, 1)
             if live(n - 1):
                 regroup_latent(n - 1)
-            if live(n):
-                normalise(n)
+            if live(n + 3):
+                regroup_x(n + 3)
+            if live(n + 2):
+                quantise_x(n + 2)
             if live(n - 1):
                 quantise_latent(n - 1)

from contextlib import ExitStack

import concourse.mybir as mybir
from concourse.masks import make_identity

F32 = mybir.dt.float32
BF16 = mybir.dt.bfloat16
U32 = mybir.dt.uint32
U8 = mybir.dt.uint8
I32 = mybir.dt.int32
FP8X4 = mybir.dt.float8_e4m3fn_x4
ADD = mybir.AluOpType.add
MULT = mybir.AluOpType.mult
ACT = mybir.ActivationFunctionType

P = 128
PACK = 4
HALVES = 2
TOKENS = 4096
K = 512
HEADS = 4
HEAD = 128
KV = 2
EPS = 1e-6

GROUP_TILES = 4
GROUPS = TOKENS // (P * GROUP_TILES)
ROUND_TILES = 2
ROUNDS = TOKENS // (P * ROUND_TILES)
ROUND_COLS = ROUND_TILES * P

BIAS_A = 0
GAIN = K
BIAS_B = 2 * K
VECTOR_COLS = 2 * K + HEADS * KV * HEAD

FLOPS = 2 * TOKENS * K * K + 2 * TOKENS * K * (HEADS * KV * HEAD)


def block(i, width):
    return slice(i * width, (i + 1) * width)


def live(r):
    return 0 <= r < ROUNDS


def tile_mla_pa_t_kernel(
    tc, x, wkv_a_w, wkv_a_b, kv_norm_w, wkv_b_w, wkv_b_b, out_0, out_1
):
    nc = tc.nc
    x_groups = x.flatten_outer_dims().rearrange("(g p i) d -> g p (i d)", p=P, i=GROUP_TILES)
    out_groups = [
        o.rearrange("b s h c -> (b s) (h c)").rearrange("(g p i) n -> g p i n", p=P, i=GROUP_TILES)
        for o in (out_0, out_1)
    ]

    with ExitStack() as stack:
        keep = stack.enter_context(tc.tile_pool(name="keep", bufs=1))
        work = stack.enter_context(tc.tile_pool(name="work", bufs=2))
        scrap = stack.enter_context(tc.tile_pool(name="scrap", bufs=4))
        stage = stack.enter_context(tc.tile_pool(name="stage", bufs=8))
        psum_t = stack.enter_context(tc.psum_pool(name="psum_t", bufs=1))
        psum_c = stack.enter_context(tc.psum_pool(name="psum_c", bufs=ROUND_TILES))
        psum_o = stack.enter_context(tc.psum_pool(name="psum_o", bufs=ROUND_TILES * KV))
        stack.enter_context(tc.manual_schedule())

        wa_sb = keep.tile([P, K // P, K], BF16)
        wb_sb = keep.tile([P, HEADS, KV, K], BF16)
        x_sb = keep.tile([P, GROUPS, GROUP_TILES * K], BF16)
        nc.sync.dma_start(out=wa_sb[:], in_=wkv_a_w.rearrange("(m p) d -> p m d", p=P))
        nc.sync.dma_start(out=x_sb[:, 0, :], in_=x_groups[0])
        wb_heads = wkv_b_w.rearrange("(h s p) r -> h p s r", s=KV, p=P)
        for h in range(HEADS):
            nc.sync.dma_start(out=wb_sb[:, h], in_=wb_heads[h])
        for g in range(1, GROUPS):
            nc.sync.dma_start(out=x_sb[:, g, :], in_=x_groups[g])

        one = keep.tile([P, 1], F32)
        nc.vector.memset(one[:], 1.0)
        nc.scalar.activation(out=one[:], in_=one[:], func=ACT.Sqrt)
        eps = keep.tile([P, 1], F32)
        nc.vector.memset(eps[:], EPS)
        ident = keep.tile([P, P], F32)
        make_identity(nc, ident[:])

        vectors = keep.tile([P, VECTOR_COLS], BF16)
        nc.vector.memset(vectors[:].bitcast(I32), 0)
        for first, vector in ((BIAS_A, wkv_a_b), (GAIN, kv_norm_w), (BIAS_B, wkv_b_b)):
            nc.scalar.dma_start(
                out=vectors[0:1, first : first + vector.shape[0]],
                in_=vector.rearrange("(o n) -> o n", o=1),
            )
        ones = keep.tile([P, P], BF16)
        nc.vector.memset(ones[:], 1.0)
        spread = keep.tile([P, VECTOR_COLS], BF16)
        bias_a = spread[:, BIAS_A : BIAS_A + K]
        gain = spread[:, GAIN : GAIN + K]
        bias_b = spread[:, BIAS_B:VECTOR_COLS].rearrange("p (h s c) -> p h s c", h=HEADS, s=KV)
        spread_banks = {}

        def spread_on_tensor(b):
            spread_banks[b] = psum_o.tile([P, K], F32, tag="o", name="spread_bank")
            nc.tensor.matmul(
                out=spread_banks[b][:], lhsT=ones[:], rhs=vectors[:, block(b, K)], start=True, stop=True
            )

        def spread_on_vector(b):
            nc.vector.tensor_copy(out=spread[:, block(b, K)], in_=spread_banks[b][:])

        def transpose_words(bank, rows):
            for s in range(len(rows)):
                words = rows[s].bitcast(F32)
                for u in range(HALVES):
                    nc.tensor.transpose(bank[:, s, u, :], words[:, block(u, P)], ident[:])

        def pair_halves(bank):
            return bank[:].rearrange("p s u r -> p s r u")

        wa_grouped = keep.tile([P, K, PACK], BF16, align_bytes=64)
        wa_codes = keep.tile([P, K], U32, align_bytes=64)
        wa_scales = keep.tile([P, K], U8, align_bytes=64)
        for b in range(2):
            wa_bank = psum_o.tile([P, 2, HALVES, P], F32, tag="o")
            transpose_words(wa_bank, [wa_sb[:, 2 * b + s, :] for s in range(2)])
            nc.scalar.copy(
                out=wa_grouped[:, block(b, 2 * P), :]
                .bitcast(F32)
                .rearrange("p (s r) u -> p s r u", s=2),
                in_=pair_halves(wa_bank),
            )
        nc.vector.quantize_mx(
            out=wa_codes[:].bitcast(FP8X4),
            scales=wa_scales[:],
            in_=wa_grouped[:].rearrange("p r j -> p (r j)"),
        )

        wb_codes = keep.tile([P, KV, HEADS, HEAD], U32, align_bytes=64)
        wb_scales = keep.tile([P, KV, HEADS, HEAD], U8, align_bytes=64)
        wb_banks = {}

        def transpose_wb(h):
            wb_banks[h] = psum_o.tile([P, KV, HALVES, P], F32, tag="o", name="wb_bank")
            transpose_words(wb_banks[h], [wb_sb[:, h, s, :] for s in range(KV)])

        def quantise_wb(h):
            wb_grouped = work.tile([P, KV, HEAD, PACK], BF16, align_bytes=64)
            nc.vector.tensor_copy(out=wb_grouped[:].bitcast(F32), in_=pair_halves(wb_banks[h]))
            for s in range(KV):
                nc.vector.quantize_mx(
                    out=wb_codes[:, s, h, :].bitcast(FP8X4),
                    scales=wb_scales[:, s, h, :],
                    in_=wb_grouped[:, s].rearrange("p r j -> p (r j)"),
                )

        x_bank, x_grouped, x_codes, x_scales = {}, {}, {}, {}
        c_bank, c_biased, c_gained, rms, rstd = {}, {}, {}, {}, {}
        l_rows, l_bank, l_grouped, l_codes, l_scales = {}, {}, {}, {}, {}
        o_bank = {}

        def transpose_x(r):
            g, first = divmod(r * ROUND_TILES, GROUP_TILES)
            x_bank[r] = psum_t.tile([P, ROUND_TILES, HALVES, P], F32, name="x_bank")
            transpose_words(
                x_bank[r], [x_sb[:, g, block(first + s, K)] for s in range(ROUND_TILES)]
            )

        def regroup_x(r):
            x_grouped[r] = work.tile(
                [P, ROUND_TILES, P, PACK], BF16, align_bytes=64, name="x_grouped"
            )
            nc.scalar.copy(out=x_grouped[r][:].bitcast(F32), in_=pair_halves(x_bank[r]))

        def quantise(grouped, codes, scales):
            nc.vector.quantize_mx(
                out=codes[:].bitcast(FP8X4),
                scales=scales[:],
                in_=grouped[:].rearrange("p s t j -> p (s t j)"),
            )

        def quantise_x(r):
            x_codes[r] = work.tile([P, ROUND_COLS], U32, align_bytes=64, name="x_codes")
            x_scales[r] = work.tile([P, ROUND_COLS], U8, align_bytes=64, name="x_scales")
            quantise(x_grouped[r], x_codes[r], x_scales[r])

        def first_matmul(r):
            for s in range(ROUND_TILES):
                c_bank[r, s] = psum_c.tile([P, K], F32, name="c_bank")
                nc.tensor.matmul_mx(
                    out=c_bank[r, s][:],
                    lhsT=x_codes[r][:, block(s, P)].bitcast(FP8X4),
                    lhsT_scale=x_scales[r][:, block(s, P)],
                    rhs=wa_codes[:].bitcast(FP8X4),
                    rhs_scale=wa_scales[:],
                    start=True,
                    stop=True,
                )

        def add_first_bias(r):
            c_biased[r] = work.tile([P, ROUND_TILES, K], F32, name="c_biased")
            for s in range(ROUND_TILES):
                nc.vector.tensor_tensor(
                    out=c_biased[r][:, s, :], in0=c_bank[r, s][:], in1=bias_a, op=ADD
                )

        def apply_gain(r):
            c_gained[r] = work.tile([P, ROUND_TILES, K], F32, name="c_gained")
            for s in range(ROUND_TILES):
                nc.gpsimd.tensor_tensor(
                    out=c_gained[r][:, s, :], in0=c_biased[r][:, s, :], in1=gain, op=MULT
                )

        def root_mean_square(r):
            sum_sq = work.tile([P, ROUND_TILES], F32, name="sum_sq")
            for s in range(ROUND_TILES):
                squares = scrap.tile([P, K], BF16, name="squares")
                nc.scalar.activation(
                    out=squares[:],
                    in_=c_biased[r][:, s, :],
                    func=ACT.Square,
                    accum_out=sum_sq[:, s : s + 1],
                )
            rms[r] = work.tile([P, ROUND_TILES], F32, name="rms")
            nc.scalar.activation(
                out=rms[r][:], in_=sum_sq[:], func=ACT.Sqrt, scale=1.0 / K, bias=eps[:]
            )

        def invert(r):
            rstd[r] = work.tile([P, ROUND_TILES], F32, name="rstd")
            nc.vector.reciprocal(out=rstd[r][:], in_=rms[r][:])

        def normalise(r):
            l_rows[r] = work.tile([P, ROUND_TILES, K], BF16, name="l_rows")
            for s in range(ROUND_TILES):
                nc.scalar.activation(
                    out=l_rows[r][:, s, :],
                    in_=c_gained[r][:, s, :],
                    func=ACT.Copy,
                    scale=rstd[r][:, s : s + 1],
                )

        def transpose_latent(r):
            l_bank[r] = psum_t.tile([P, ROUND_TILES, HALVES, P], F32, name="l_bank")
            transpose_words(l_bank[r], [l_rows[r][:, s, :] for s in range(ROUND_TILES)])

        def regroup_latent(r):
            l_grouped[r] = work.tile(
                [P, ROUND_TILES, P, PACK], BF16, align_bytes=64, name="l_grouped"
            )
            nc.scalar.copy(out=l_grouped[r][:].bitcast(F32), in_=pair_halves(l_bank[r]))

        def quantise_latent(r):
            l_codes[r] = work.tile([P, ROUND_COLS], U32, align_bytes=64, name="l_codes")
            l_scales[r] = work.tile([P, ROUND_COLS], U8, align_bytes=64, name="l_scales")
            quantise(l_grouped[r], l_codes[r], l_scales[r])

        def second_matmul(r):
            for kv in range(KV):
                for s in range(ROUND_TILES):
                    o_bank[r, s, kv] = psum_o.tile([P, HEADS, HEAD], F32, tag="o", name="o_bank")
                    nc.tensor.matmul_mx(
                        out=o_bank[r, s, kv][:].rearrange("p h c -> p (h c)"),
                        lhsT=l_codes[r][:, block(s, P)].bitcast(FP8X4),
                        lhsT_scale=l_scales[r][:, block(s, P)],
                        rhs=wb_codes[:, kv].rearrange("p h c -> p (h c)").bitcast(FP8X4),
                        rhs_scale=wb_scales[:, kv].rearrange("p h c -> p (h c)"),
                        start=True,
                        stop=True,
                    )

        def add_second_bias_and_store(r, kv):
            g, first = divmod(r * ROUND_TILES, GROUP_TILES)
            result = stage.tile([P, ROUND_TILES, HEADS, HEAD], F32, name="result")
            for s in range(ROUND_TILES):
                nc.vector.tensor_tensor(
                    out=result[:, s], in0=o_bank[r, s, kv][:], in1=bias_b[:, :, kv, :], op=ADD
                )
            nc.sync.dma_start(
                out=out_groups[kv][g][:, first : first + ROUND_TILES, :],
                in_=result[:].rearrange("p s h c -> p s (h c)"),
            )

        for n in range(-3, ROUNDS + 2):
            if live(n):
                add_first_bias(n)
            if live(n - 1):
                normalise(n - 1)
            if live(n - 2):
                second_matmul(n - 2)
            elif n == -2:
                spread_on_tensor(0)
                spread_on_tensor(1)
            elif n >= 0:
                transpose_wb(2 * n)
                transpose_wb(2 * n + 1)
                spread_on_tensor(2 + n)
            if live(n + 1):
                first_matmul(n + 1)
            if live(n - 1):
                transpose_latent(n - 1)
            if live(n + 3):
                transpose_x(n + 3)
            if live(n):
                apply_gain(n)
            if live(n - 2):
                add_second_bias_and_store(n - 2, 0)
                add_second_bias_and_store(n - 2, 1)
            elif n == -2:
                spread_on_vector(0)
                spread_on_vector(1)
            elif n >= 0:
                quantise_wb(2 * n)
                quantise_wb(2 * n + 1)
                spread_on_vector(2 + n)
            if live(n):
                root_mean_square(n)
                invert(n)
            if live(n - 1):
                regroup_latent(n - 1)
            if live(n + 3):
                regroup_x(n + 3)
            if live(n + 2):
                quantise_x(n + 2)
            if live(n - 1):
                quantise_latent(n - 1)
